import numpy as np
import ml_dtypes


def mxq(x, axis, fmt="e4m3"):
    dtype, down = {"e4m3": (ml_dtypes.float8_e4m3fn, 7), "e5m2": (ml_dtypes.float8_e5m2, 14)}[fmt]
    v = np.moveaxis(np.asarray(x, np.float32).astype(ml_dtypes.bfloat16).astype(np.float64), axis, -1)
    blocks = v.reshape(v.shape[:-1] + (-1, 32))
    amax = np.abs(blocks).max(-1, keepdims=True)
    byte = np.maximum(np.where(amax > 0, np.frexp(amax)[1] - 1 + 127, 0) - down, 1)
    scale = np.exp2(byte - 127.0)
    codes = (blocks / scale).astype(np.float32).astype(dtype).astype(np.float64)
    return np.moveaxis((codes * scale).reshape(v.shape), -1, axis)


WIDE = False


def mx_kscale(k):
    if not WIDE:
        return np.ones(k)
    levels = np.array([10, -10, 5, -5, 0])
    if k % 512:
        return np.exp2(np.random.permutation(np.resize(levels, k // 32))).repeat(32)
    a = np.empty((k // 512, 16))
    for p in range(k // 512):
        a[p, :8] = np.random.permutation(np.resize(levels, 8))
        for g in range(8):
            far = levels[np.abs(levels - a[p, g]) >= 10]
            a[p, g + 8] = far[np.random.randint(len(far))]
    return np.exp2(a.ravel()).repeat(32)


BF16 = ml_dtypes.bfloat16


def bf(x):
    return np.asarray(x, np.float32).astype(BF16)


def f64(x):
    return np.asarray(x).astype(np.float64)


B, LC, LL, LLAMA_DIM, DIM, HEADS, FF = 4, 77, 64, 2048, 1536, 16, 6144
EPS = 1e-5


def layernorm(x, g, b):
    m = x.mean(-1, keepdims=True)
    v = ((x - m) ** 2).mean(-1, keepdims=True)
    return (x - m) / np.sqrt(v + EPS) * g + b


def setup_inputs():
    s, t = mx_kscale(LLAMA_DIM), mx_kscale(DIM)
    return {
        "llm_embed": bf(np.random.standard_normal((B, LL, LLAMA_DIM)) * s),
        "llm_proj_w": bf(np.random.standard_normal((DIM, LLAMA_DIM)) / np.sqrt(LLAMA_DIM) / s),
        "llm_proj_b": bf(0.1 * np.random.standard_normal(DIM)),
        "kvn_g": bf((1.0 + 0.1 * np.random.standard_normal(DIM)) * t),
        "kvn_b": bf(0.1 * np.random.standard_normal(DIM) * t),
        "q_w": bf(np.random.standard_normal((DIM, DIM)) / np.sqrt(DIM) / t),
        "q_b": bf(0.1 * np.random.standard_normal(DIM)),
    }


def reference(llm_embed, llm_proj_w, llm_proj_b, kvn_g, kvn_b, q_w, q_b):
    llm = (mxq(f64(llm_embed), 2, "e4m3") @ mxq(f64(llm_proj_w), 1, "e4m3").T) + f64(llm_proj_b)
    llm_n = layernorm(llm, f64(kvn_g), f64(kvn_b))
    q = (mxq(llm_n, 2, "e4m3") @ mxq(f64(q_w), 1, "e4m3").T) + f64(q_b)
    return llm, q

@@ -1,0 +1,255 @@
+import concourse.mybir as mybir
+from concourse.masks import make_identity
+
+F32 = mybir.dt.float32
+BF16 = mybir.dt.bfloat16
+U32 = mybir.dt.uint32
+U8 = mybir.dt.uint8
+I32 = mybir.dt.int32
+FP8X4 = mybir.dt.float8_e4m3fn_x4
+ALU = mybir.AluOpType
+ACT = mybir.ActivationFunctionType
+
+P = 128
+PACK = 4
+K_PASS = P * PACK
+ROWS = 2 * P
+TOKENS = 256
+TOKEN_TILES = TOKENS // P
+K1 = 2048
+DIM = 1536
+PASSES1 = K1 // K_PASS
+PASSES2 = DIM // K_PASS
+UNITS = DIM // ROWS
+BANK = 512
+CHUNKS = DIM // BANK
+EPS = 1e-5
+
+FLOPS = 2 * TOKENS * K1 * DIM + 2 * TOKENS * DIM * DIM
+
+
+def tile_crossfusion_pa_kernel(
+    tc, llm_embed, llm_proj_w, llm_proj_b, kvn_g, kvn_b, q_w, q_b, out_0, out_1
+):
+    nc = tc.nc
+    x_rows = llm_embed.flatten_outer_dims()
+    llm_out = out_0.flatten_outer_dims()
+    q_out = out_1.flatten_outer_dims()
+
+    with tc.tile_pool(name="keep", bufs=1) as keep, tc.tile_pool(
+        name="stage", bufs=6
+    ) as stage, tc.tile_pool(name="w1q", bufs=3) as w1q, tc.psum_pool(
+        name="psum", bufs=8
+    ) as psum:
+
+        def load_unit(rows, width, name):
+            raw = keep.tile([P, 2, width], BF16, name=name)
+            nc.sync.dma_start(out=raw[:], in_=rows.rearrange("(r p) k -> p r k", p=P))
+            return raw
+
+        b1_rows = keep.tile([P, DIM], BF16)
+        nc.vector.memset(b1_rows[:].bitcast(I32), 0)
+        gb_rows = keep.tile([P, K_PASS], BF16)
+        nc.vector.memset(gb_rows[:].bitcast(I32), 0)
+        ones = keep.tile([P, P], BF16)
+        nc.vector.memset(ones[:], 1.0)
+        eps = keep.tile([P, 1], F32)
+        nc.vector.memset(eps[:], EPS)
+        ident = keep.tile([P, P], F32)
+        make_identity(nc, ident[:])
+        warm = keep.tile([P, 1], F32)
+        nc.scalar.activation(out=warm[:], in_=eps[:], func=ACT.Sqrt)
+
+        x_raw = load_unit(x_rows, K1, "x_raw")
+        nc.sync.dma_start(out=b1_rows[0:1, :], in_=llm_proj_b.rearrange("(o n) -> o n", o=1))
+        nc.sync.dma_start(out=gb_rows[0:PASSES2, :], in_=kvn_g.rearrange("(g w) -> g w", w=K_PASS))
+        nc.sync.dma_start(out=gb_rows[PASSES2 : 2 * PASSES2, :], in_=kvn_b.rearrange("(g w) -> g w", w=K_PASS))
+        w1_raw = [load_unit(llm_proj_w[u * ROWS : (u + 1) * ROWS, :], K1, "w1_raw%d" % u) for u in range(UNITS)]
+        w2_raw = [load_unit(q_w[u * ROWS : (u + 1) * ROWS, :], DIM, "w2_raw%d" % u) for u in range(UNITS)]
+        qb_all = keep.tile([P, DIM], BF16)
+        nc.sync.dma_start(out=qb_all[:], in_=q_b.partition_broadcast(P))
+
+        def transpose_unit(raw, passes):
+            grouped_tiles = []
+            for g in range(passes):
+                bank = psum.tile([P, 2, ROWS], F32, tag="bank", name="bank")
+                for u in range(2):
+                    for r in range(2):
+                        nc.tensor.transpose(
+                            bank[:, u, r * P : (r + 1) * P],
+                            raw[:, r, :].bitcast(F32)[:, g * ROWS + u : (g + 1) * ROWS : 2],
+                            ident[:],
+                        )
+                grouped = stage.tile([P, ROWS * PACK], BF16, align_bytes=64, tag="grouped", name="grouped")
+                nc.scalar.copy(
+                    out=grouped[:].bitcast(F32).rearrange("p (c u) -> p c u", u=2),
+                    in_=bank[:].rearrange("p u c -> p c u"),
+                )
+                grouped_tiles.append(grouped)
+            return grouped_tiles
+
+        def quantise_unit(grouped_tiles, codes, scales, cols):
+            for g, grouped in enumerate(grouped_tiles):
+                nc.vector.quantize_mx(
+                    out=codes[:, g, cols].bitcast(FP8X4), scales=scales[:, g, cols], in_=grouped[:]
+                )
+
+        x_codes = keep.tile([P, PASSES1, TOKENS], U32, align_bytes=64)
+        x_scales = keep.tile([P, PASSES1, TOKENS], U8, align_bytes=64)
+        w2_codes = keep.tile([P, PASSES2, DIM], U32, align_bytes=64)
+        w2_scales = keep.tile([P, PASSES2, DIM], U8, align_bytes=64)
+        b1_all = keep.tile([P, DIM], BF16)
+        llm = keep.tile([P, TOKEN_TILES, DIM], F32)
+        stats = keep.tile([P, TOKEN_TILES, UNITS, 6], F32)
+
+        def quantise_w1(grouped_tiles):
+            w1_codes = w1q.tile([P, PASSES1, ROWS], U32, align_bytes=64, name="w1_codes")
+            w1_scales = w1q.tile([P, PASSES1, ROWS], U8, align_bytes=64, name="w1_scales")
+            quantise_unit(grouped_tiles, w1_codes, w1_scales, slice(0, ROWS))
+            return w1_codes, w1_scales
+
+        def quantise_w2(u, grouped_tiles):
+            quantise_unit(grouped_tiles, w2_codes, w2_scales, slice(u * ROWS, (u + 1) * ROWS))
+
+        def first_matmul(u, w1_codes, w1_scales):
+            acc = psum.tile([P, TOKEN_TILES, ROWS], F32, tag="bank", name="acc")
+            for i in range(TOKEN_TILES):
+                tokens = slice(i * P, (i + 1) * P)
+                for g in range(PASSES1):
+                    nc.tensor.matmul_mx(
+                        out=acc[:, i, :],
+                        lhsT=x_codes[:, g, tokens].bitcast(FP8X4),
+                        lhsT_scale=x_scales[:, g, tokens],
+                        rhs=w1_codes[:, g, :].bitcast(FP8X4),
+                        rhs_scale=w1_scales[:, g, :],
+                        start=(g == 0),
+                        stop=(g == PASSES1 - 1),
+                    )
+            cols = slice(u * ROWS, (u + 1) * ROWS)
+            nc.vector.tensor_tensor(
+                out=llm[:, :, cols],
+                in0=acc[:],
+                in1=b1_all[:, cols].unsqueeze(1).to_broadcast([P, TOKEN_TILES, ROWS]),
+                op=ALU.add,
+            )
+
+        def statistics(u):
+            for i in range(TOKEN_TILES):
+                nc.vector.bn_stats(out=stats[:, i, u, :], in_=llm[:, i, u * ROWS : (u + 1) * ROWS])
+
+        quantise_unit(transpose_unit(x_raw, PASSES1), x_codes, x_scales, slice(0, TOKENS))
+
+        for c in range(CHUNKS):
+            bank = psum.tile([P, BANK], F32, tag="bank", name="bank")
+            nc.tensor.matmul(
+                out=bank[:], lhsT=ones[:], rhs=b1_rows[:, c * BANK : (c + 1) * BANK], start=True, stop=True
+            )
+            nc.vector.tensor_copy(out=b1_all[:, c * BANK : (c + 1) * BANK], in_=bank[:])
+        gb_bank = psum.tile([P, 2, P], F32, tag="bank", name="bank")
+        for u in range(2):
+            nc.tensor.transpose(gb_bank[:, u, :], gb_rows[:].bitcast(F32)[:, u::2], ident[:])
+        gb_col = keep.tile([P, 2, PASSES2, PACK], F32)
+        for u in range(2):
+            nc.vector.tensor_copy(
+                out=gb_col[:, :, :, 2 * u : 2 * u + 2].rearrange("p v g e -> p (v g) e"),
+                in_=gb_bank[:, u, 0 : 2 * PASSES2].bitcast(BF16).rearrange("p (w e) -> p w e", e=2),
+            )
+
+        ready = quantise_w1(transpose_unit(w1_raw[0], PASSES1))
+        for u in range(UNITS):
+            if u + 1 < UNITS:
+                following = quantise_w1(transpose_unit(w1_raw[u + 1], PASSES1))
+            else:
+                quantise_w2(0, transpose_unit(w2_raw[0], PASSES2))
+            if u > 0:
+                statistics(u - 1)
+            first_matmul(u, ready[0], ready[1])
+            ready = following
+        statistics(UNITS - 1)
+        for i in range(TOKEN_TILES):
+            nc.sync.dma_start(out=llm_out[i * P : (i + 1) * P, :], in_=llm[:, i, :])
+
+        w2_grouped = transpose_unit(w2_raw[1], PASSES2)
+        mean_var = keep.tile([P, TOKEN_TILES, 2], F32)
+        for i in range(TOKEN_TILES):
+            nc.vector.bn_aggr(out=mean_var[:, i, :], in_=stats[:, i, :, :].rearrange("p u s -> p (u s)"))
+        std = keep.tile([P, TOKEN_TILES], F32)
+        nc.scalar.activation(out=std[:], in_=mean_var[:, :, 1], func=ACT.Sqrt, bias=eps[:, 0:1], scale=1.0)
+        rstd = keep.tile([P, TOKEN_TILES], F32)
+        nc.vector.reciprocal(out=rstd[:], in_=std[:])
+        offset = keep.tile([P, TOKEN_TILES], F32)
+        nc.vector.scalar_tensor_tensor(
+            out=offset[:], in0=mean_var[:, :, 0], scalar=-1.0, in1=rstd[:], op0=ALU.mult, op1=ALU.mult
+        )
+
+        xhat = keep.tile([P, TOKEN_TILES, PASSES2, PACK, P], F32)
+        for g in range(PASSES2):
+            for i in range(TOKEN_TILES):
+                source = llm[:, i, g * K_PASS : (g + 1) * K_PASS].rearrange("n (p t) -> n t p", t=PACK)
+                target = xhat[:, i, g, :, :]
+                if i == 0:
+                    nc.vector.tensor_scalar(
+                        out=target, in0=source, scalar1=rstd[:, i : i + 1], scalar2=offset[:, i : i + 1],
+                        op0=ALU.mult, op1=ALU.add,
+                    )
+                else:
+                    nc.scalar.activation(
+                        out=target, in_=source, func=ACT.Identity, scale=rstd[:, i : i + 1], bias=offset[:, i : i + 1]
+                    )
+        quantise_w2(1, w2_grouped)
+
+        n_codes = keep.tile([P, PASSES2, TOKENS], U32, align_bytes=64)
+        n_scales = keep.tile([P, PASSES2, TOKENS], U8, align_bytes=64)
+        n_grouped = []
+        for g in range(PASSES2):
+            planes = stage.tile([P, PACK, TOKENS], BF16, tag="planes", name="planes", bufs=2)
+            for u in range(2):
+                bank = psum.tile([P, 2, TOKENS], F32, tag="bank", name="bank")
+                for e in range(2):
+                    for i in range(TOKEN_TILES):
+                        nc.tensor.transpose(bank[:, e, i * P : (i + 1) * P], xhat[:, i, g, 2 * u + e, :], ident[:])
+                for e in range(2):
+                    gain = gb_col[:, 0, g, 2 * u + e : 2 * u + e + 1]
+                    shift = gb_col[:, 1, g, 2 * u + e : 2 * u + e + 1]
+                    if u == 0:
+                        nc.scalar.activation(
+                            out=planes[:, 2 * u + e, :], in_=bank[:, e, :], func=ACT.Identity, scale=gain, bias=shift
+                        )
+                    else:
+                        nc.vector.tensor_scalar(
+                            out=planes[:, 2 * u + e, :], in0=bank[:, e, :], scalar1=gain, scalar2=shift,
+                            op0=ALU.mult, op1=ALU.add,
+                        )
+            grouped = stage.tile([P, TOKENS * PACK], BF16, align_bytes=64, tag="n_grouped", name="n_grouped", bufs=3)
+            nc.vector.tensor_copy(
+                out=grouped[:].rearrange("p (r t) -> p r t", t=PACK), in_=planes[:].rearrange("p t r -> p r t")
+            )
+            n_grouped.append(grouped)
+            if g > 0:
+                nc.vector.quantize_mx(
+                    out=n_codes[:, g - 1, :].bitcast(FP8X4), scales=n_scales[:, g - 1, :], in_=n_grouped[g - 1][:]
+                )
+        last = PASSES2 - 1
+        nc.vector.quantize_mx(out=n_codes[:, last, :].bitcast(FP8X4), scales=n_scales[:, last, :], in_=n_grouped[last][:])
+
+        for u in range(2, UNITS):
+            quantise_w2(u, transpose_unit(w2_raw[u], PASSES2))
+
+        q_sb = keep.tile([P, TOKEN_TILES, DIM], F32)
+        for c in range(CHUNKS):
+            cols = slice(c * BANK, (c + 1) * BANK)
+            for i in range(TOKEN_TILES):
+                tokens = slice(i * P, (i + 1) * P)
+                acc = psum.tile([P, BANK], F32, tag="bank", name="acc")
+                for g in range(PASSES2):
+                    nc.tensor.matmul_mx(
+                        out=acc[:],
+                        lhsT=n_codes[:, g, tokens].bitcast(FP8X4),
+                        lhsT_scale=n_scales[:, g, tokens],
+                        rhs=w2_codes[:, g, cols].bitcast(FP8X4),
+                        rhs_scale=w2_scales[:, g, cols],
+                        start=(g == 0),
+                        stop=(g == PASSES2 - 1),
+                    )
+                nc.vector.tensor_tensor(out=q_sb[:, i, cols], in0=acc[:], in1=qb_all[:, cols], op=ALU.add)
+                nc.sync.dma_start(out=q_out[i * P : (i + 1) * P, cols], in_=q_sb[:, i, cols])

@@ -42,15 +42,19 @@ def tile_crossfusion_pa_kernel(
         name="psum", bufs=8
     ) as psum:
 
-        def load_unit(rows, width, name):
-            raw = keep.tile([P, 2, width], BF16, name=name)
-            nc.sync.dma_start(out=raw[:], in_=rows.rearrange("(r p) k -> p r k", p=P))
-            return raw
+        def load_unit(rows, width, name, parts=1):
+            pieces = []
+            step = width // parts
+            for c in range(parts):
+                raw = keep.tile([P, 2, step], BF16, name="%s_%d" % (name, c))
+                nc.sync.dma_start(
+                    out=raw[:], in_=rows[:, c * step : (c + 1) * step].rearrange("(r p) k -> p r k", p=P)
+                )
+                pieces.append(raw)
+            return pieces
 
         b1_rows = keep.tile([P, DIM], BF16)
         nc.vector.memset(b1_rows[:].bitcast(I32), 0)
-        gb_rows = keep.tile([P, K_PASS], BF16)
-        nc.vector.memset(gb_rows[:].bitcast(I32), 0)
         ones = keep.tile([P, P], BF16)
         nc.vector.memset(ones[:], 1.0)
         eps = keep.tile([P, 1], F32)
@@ -60,24 +64,29 @@ def tile_crossfusion_pa_kernel(
         warm = keep.tile([P, 1], F32)
         nc.scalar.activation(out=warm[:], in_=eps[:], func=ACT.Sqrt)
 
-        x_raw = load_unit(x_rows, K1, "x_raw")
-        nc.sync.dma_start(out=b1_rows[0:1, :], in_=llm_proj_b.rearrange("(o n) -> o n", o=1))
-        nc.sync.dma_start(out=gb_rows[0:PASSES2, :], in_=kvn_g.rearrange("(g w) -> g w", w=K_PASS))
-        nc.sync.dma_start(out=gb_rows[PASSES2 : 2 * PASSES2, :], in_=kvn_b.rearrange("(g w) -> g w", w=K_PASS))
-        w1_raw = [load_unit(llm_proj_w[u * ROWS : (u + 1) * ROWS, :], K1, "w1_raw%d" % u) for u in range(UNITS)]
+        x_raw = load_unit(x_rows, K1, "x_raw", 2)
+        nc.scalar.dma_start(out=b1_rows[0:1, :], in_=llm_proj_b.rearrange("(o n) -> o n", o=1))
+        gain_raw = keep.tile([P, PASSES2, PACK], BF16)
+        nc.scalar.dma_start(out=gain_raw[:], in_=kvn_g.rearrange("(g p t) -> p g t", p=P, t=PACK))
+        shift_raw = keep.tile([P, PASSES2, PACK], BF16)
+        nc.scalar.dma_start(out=shift_raw[:], in_=kvn_b.rearrange("(g p t) -> p g t", p=P, t=PACK))
+        w1_raw = [load_unit(llm_proj_w[u * ROWS : (u + 1) * ROWS, :], K1, "w1_raw%d" % u, 2 if u < 2 else 1) for u in range(UNITS)]
         w2_raw = [load_unit(q_w[u * ROWS : (u + 1) * ROWS, :], DIM, "w2_raw%d" % u) for u in range(UNITS)]
         qb_all = keep.tile([P, DIM], BF16)
         nc.sync.dma_start(out=qb_all[:], in_=q_b.partition_broadcast(P))
 
         def transpose_unit(raw, passes):
             grouped_tiles = []
+            in_tile = passes // len(raw)
             for g in range(passes):
+                words = raw[g // in_tile]
+                first = (g % in_tile) * ROWS
                 bank = psum.tile([P, 2, ROWS], F32, tag="bank", name="bank")
                 for u in range(2):
                     for r in range(2):
                         nc.tensor.transpose(
                             bank[:, u, r * P : (r + 1) * P],
-                            raw[:, r, :].bitcast(F32)[:, g * ROWS + u : (g + 1) * ROWS : 2],
+                            words[:, r, :].bitcast(F32)[:, first + u : first + ROWS : 2],
                             ident[:],
                         )
                 grouped = stage.tile([P, ROWS * PACK], BF16, align_bytes=64, tag="grouped", name="grouped")
@@ -139,23 +148,18 @@ def tile_crossfusion_pa_kernel(
 
         quantise_unit(transpose_unit(x_raw, PASSES1), x_codes, x_scales, slice(0, TOKENS))
 
+        ready = quantise_w1(transpose_unit(w1_raw[0], PASSES1))
         for c in range(CHUNKS):
             bank = psum.tile([P, BANK], F32, tag="bank", name="bank")
             nc.tensor.matmul(
                 out=bank[:], lhsT=ones[:], rhs=b1_rows[:, c * BANK : (c + 1) * BANK], start=True, stop=True
             )
             nc.vector.tensor_copy(out=b1_all[:, c * BANK : (c + 1) * BANK], in_=bank[:])
-        gb_bank = psum.tile([P, 2, P], F32, tag="bank", name="bank")
-        for u in range(2):
-            nc.tensor.transpose(gb_bank[:, u, :], gb_rows[:].bitcast(F32)[:, u::2], ident[:])
-        gb_col = keep.tile([P, 2, PASSES2, PACK], F32)
-        for u in range(2):
-            nc.vector.tensor_copy(
-                out=gb_col[:, :, :, 2 * u : 2 * u + 2].rearrange("p v g e -> p (v g) e"),
-                in_=gb_bank[:, u, 0 : 2 * PASSES2].bitcast(BF16).rearrange("p (w e) -> p w e", e=2),
-            )
+        gain = keep.tile([P, PASSES2, PACK], F32)
+        nc.vector.tensor_copy(out=gain[:], in_=gain_raw[:])
+        shift = keep.tile([P, PASSES2, PACK], F32)
+        nc.vector.tensor_copy(out=shift[:], in_=shift_raw[:])
 
-        ready = quantise_w1(transpose_unit(w1_raw[0], PASSES1))
         for u in range(UNITS):
             if u + 1 < UNITS:
                 following = quantise_w1(transpose_unit(w1_raw[u + 1], PASSES1))
@@ -169,7 +173,7 @@ def tile_crossfusion_pa_kernel(
         for i in range(TOKEN_TILES):
             nc.sync.dma_start(out=llm_out[i * P : (i + 1) * P, :], in_=llm[:, i, :])
 
-        w2_grouped = transpose_unit(w2_raw[1], PASSES2)
+        w2_grouped = [transpose_unit(w2_raw[u], PASSES2) for u in (1, 2)]
         mean_var = keep.tile([P, TOKEN_TILES, 2], F32)
         for i in range(TOKEN_TILES):
             nc.vector.bn_aggr(out=mean_var[:, i, :], in_=stats[:, i, :, :].rearrange("p u s -> p (u s)"))
@@ -185,8 +189,8 @@ def tile_crossfusion_pa_kernel(
         xhat = keep.tile([P, TOKEN_TILES, PASSES2, PACK, P], F32)
         for g in range(PASSES2):
             for i in range(TOKEN_TILES):
-                source = llm[:, i, g * K_PASS : (g + 1) * K_PASS].rearrange("n (p t) -> n t p", t=PACK)
-                target = xhat[:, i, g, :, :]
+                source = llm[:, i, g * K_PASS : (g + 1) * K_PASS].rearrange("n (p t) -> n p t", t=PACK)
+                target = xhat[:, i, g, :, :].rearrange("n t p -> n p t")
                 if i == 0:
                     nc.vector.tensor_scalar(
                         out=target, in0=source, scalar1=rstd[:, i : i + 1], scalar2=offset[:, i : i + 1],
@@ -196,7 +200,8 @@ def tile_crossfusion_pa_kernel(
                     nc.scalar.activation(
                         out=target, in_=source, func=ACT.Identity, scale=rstd[:, i : i + 1], bias=offset[:, i : i + 1]
                     )
-        quantise_w2(1, w2_grouped)
+        quantise_w2(1, w2_grouped[0])
+        quantise_w2(2, w2_grouped[1])
 
         n_codes = keep.tile([P, PASSES2, TOKENS], U32, align_bytes=64)
         n_scales = keep.tile([P, PASSES2, TOKENS], U8, align_bytes=64)
@@ -209,16 +214,16 @@ def tile_crossfusion_pa_kernel(
                     for i in range(TOKEN_TILES):
                         nc.tensor.transpose(bank[:, e, i * P : (i + 1) * P], xhat[:, i, g, 2 * u + e, :], ident[:])
                 for e in range(2):
-                    gain = gb_col[:, 0, g, 2 * u + e : 2 * u + e + 1]
-                    shift = gb_col[:, 1, g, 2 * u + e : 2 * u + e + 1]
+                    t = 2 * u + e
                     if u == 0:
                         nc.scalar.activation(
-                            out=planes[:, 2 * u + e, :], in_=bank[:, e, :], func=ACT.Identity, scale=gain, bias=shift
+                            out=planes[:, t, :], in_=bank[:, e, :], func=ACT.Identity,
+                            scale=gain[:, g, t : t + 1], bias=shift[:, g, t : t + 1],
                         )
                     else:
                         nc.vector.tensor_scalar(
-                            out=planes[:, 2 * u + e, :], in0=bank[:, e, :], scalar1=gain, scalar2=shift,
-                            op0=ALU.mult, op1=ALU.add,
+                            out=planes[:, t, :], in0=bank[:, e, :], scalar1=gain[:, g, t : t + 1],
+                            scalar2=shift[:, g, t : t + 1], op0=ALU.mult, op1=ALU.add,
                         )
             grouped = stage.tile([P, TOKENS * PACK], BF16, align_bytes=64, tag="n_grouped", name="n_grouped", bufs=3)
             nc.vector.tensor_copy(
@@ -232,11 +237,11 @@ def tile_crossfusion_pa_kernel(
         last = PASSES2 - 1
         nc.vector.quantize_mx(out=n_codes[:, last, :].bitcast(FP8X4), scales=n_scales[:, last, :], in_=n_grouped[last][:])
 
-        for u in range(2, UNITS):
-            quantise_w2(u, transpose_unit(w2_raw[u], PASSES2))
-
+        quantise_w2(3, transpose_unit(w2_raw[3], PASSES2))
         q_sb = keep.tile([P, TOKEN_TILES, DIM], F32)
         for c in range(CHUNKS):
+            if c + 4 < UNITS:
+                quantise_w2(c + 4, transpose_unit(w2_raw[c + 4], PASSES2))
             cols = slice(c * BANK, (c + 1) * BANK)
             for i in range(TOKEN_TILES):
                 tokens = slice(i * P, (i + 1) * P)

@@ -37,10 +37,10 @@ def tile_crossfusion_pa_kernel(
     q_out = out_1.flatten_outer_dims()
 
     with tc.tile_pool(name="keep", bufs=1) as keep, tc.tile_pool(
-        name="stage", bufs=6
+        name="stage", bufs=8
     ) as stage, tc.tile_pool(name="w1q", bufs=3) as w1q, tc.psum_pool(
         name="psum", bufs=8
-    ) as psum:
+    ) as psum, tc.manual_schedule():
 
         def load_unit(rows, width, name, parts=1):
             pieces = []
@@ -53,40 +53,62 @@ def tile_crossfusion_pa_kernel(
                 pieces.append(raw)
             return pieces
 
-        b1_rows = keep.tile([P, DIM], BF16)
-        nc.vector.memset(b1_rows[:].bitcast(I32), 0)
+        x_raw = load_unit(x_rows, K1, "x_raw", 2)
         ones = keep.tile([P, P], BF16)
         nc.vector.memset(ones[:], 1.0)
-        eps = keep.tile([P, 1], F32)
-        nc.vector.memset(eps[:], EPS)
-        ident = keep.tile([P, P], F32)
-        make_identity(nc, ident[:])
-        warm = keep.tile([P, 1], F32)
-        nc.scalar.activation(out=warm[:], in_=eps[:], func=ACT.Sqrt)
-
-        x_raw = load_unit(x_rows, K1, "x_raw", 2)
+        b1_rows = keep.tile([P, DIM], BF16)
+        nc.vector.memset(b1_rows[:].bitcast(I32), 0)
         nc.scalar.dma_start(out=b1_rows[0:1, :], in_=llm_proj_b.rearrange("(o n) -> o n", o=1))
         gain_raw = keep.tile([P, PASSES2, PACK], BF16)
         nc.scalar.dma_start(out=gain_raw[:], in_=kvn_g.rearrange("(g p t) -> p g t", p=P, t=PACK))
         shift_raw = keep.tile([P, PASSES2, PACK], BF16)
         nc.scalar.dma_start(out=shift_raw[:], in_=kvn_b.rearrange("(g p t) -> p g t", p=P, t=PACK))
-        w1_raw = [load_unit(llm_proj_w[u * ROWS : (u + 1) * ROWS, :], K1, "w1_raw%d" % u, 2 if u < 2 else 1) for u in range(UNITS)]
+        w1_raw = [
+            load_unit(llm_proj_w[u * ROWS : (u + 1) * ROWS, :], K1, "w1_raw%d" % u, 2 if u < 2 else 1)
+            for u in range(UNITS)
+        ]
         w2_raw = [load_unit(q_w[u * ROWS : (u + 1) * ROWS, :], DIM, "w2_raw%d" % u) for u in range(UNITS)]
         qb_all = keep.tile([P, DIM], BF16)
         nc.sync.dma_start(out=qb_all[:], in_=q_b.partition_broadcast(P))
 
-        def transpose_unit(raw, passes):
+        ident = keep.tile([P, P], F32)
+        make_identity(nc, ident[:])
+        eps = keep.tile([P, 1], F32)
+        nc.vector.memset(eps[:], EPS)
+        warm = keep.tile([P, 1], F32)
+        nc.scalar.activation(out=warm[:], in_=eps[:], func=ACT.Sqrt)
+        gain = keep.tile([P, PASSES2, PACK], F32)
+        nc.gpsimd.tensor_copy(out=gain[:], in_=gain_raw[:])
+        shift = keep.tile([P, PASSES2, PACK], F32)
+        nc.gpsimd.tensor_copy(out=shift[:], in_=shift_raw[:])
+
+        def gather_unit(raw, passes, engines):
+            gathered_tiles = []
+            in_tile = passes // len(raw)
+            for g in range(passes):
+                if engines[g] is None:
+                    gathered_tiles.append(None)
+                    continue
+                first = (g % in_tile) * ROWS
+                words = raw[g // in_tile][:].bitcast(F32)[:, :, first : first + ROWS]
+                gathered = stage.tile([P, 2, 2, P], F32, tag="gathered", name="gathered")
+                engines[g](out=gathered[:], in_=words.rearrange("p r (m u) -> p r u m", u=2))
+                gathered_tiles.append(gathered)
+            return gathered_tiles
+
+        def transpose_unit(raw, passes, gathered_tiles):
             grouped_tiles = []
             in_tile = passes // len(raw)
             for g in range(passes):
-                words = raw[g // in_tile]
+                words = raw[g // in_tile][:].bitcast(F32)
                 first = (g % in_tile) * ROWS
+                gathered = gathered_tiles[g]
                 bank = psum.tile([P, 2, ROWS], F32, tag="bank", name="bank")
                 for u in range(2):
                     for r in range(2):
                         nc.tensor.transpose(
                             bank[:, u, r * P : (r + 1) * P],
-                            words[:, r, :].bitcast(F32)[:, first + u : first + ROWS : 2],
+                            gathered[:, r, u, :] if gathered is not None else words[:, r, first + u : first + ROWS : 2],
                             ident[:],
                         )
                 grouped = stage.tile([P, ROWS * PACK], BF16, align_bytes=64, tag="grouped", name="grouped")
@@ -146,25 +168,34 @@ def tile_crossfusion_pa_kernel(
             for i in range(TOKEN_TILES):
                 nc.vector.bn_stats(out=stats[:, i, u, :], in_=llm[:, i, u * ROWS : (u + 1) * ROWS])
 
-        quantise_unit(transpose_unit(x_raw, PASSES1), x_codes, x_scales, slice(0, TOKENS))
+        def gather_w1(u):
+            return gather_unit(w1_raw[u], PASSES1, (nc.vector.tensor_copy, None, nc.scalar.copy, None))
 
-        ready = quantise_w1(transpose_unit(w1_raw[0], PASSES1))
+        def gather_w2(u):
+            return gather_unit(w2_raw[u], PASSES2, ((nc.vector.tensor_copy, None, None), (nc.vector.tensor_copy, None, None), (None, None, None), (None, None, None), (None, None, None), (None, None, None))[u])
+
+        quantise_unit(transpose_unit(x_raw, PASSES1, [None] * PASSES1), x_codes, x_scales, slice(0, TOKENS))
+        ready = quantise_w1(transpose_unit(w1_raw[0], PASSES1, [None] * PASSES1))
+        w1_gathered = gather_w1(1)
+
         for c in range(CHUNKS):
             bank = psum.tile([P, BANK], F32, tag="bank", name="bank")
             nc.tensor.matmul(
                 out=bank[:], lhsT=ones[:], rhs=b1_rows[:, c * BANK : (c + 1) * BANK], start=True, stop=True
             )
             nc.vector.tensor_copy(out=b1_all[:, c * BANK : (c + 1) * BANK], in_=bank[:])
-        gain = keep.tile([P, PASSES2, PACK], F32)
-        nc.vector.tensor_copy(out=gain[:], in_=gain_raw[:])
-        shift = keep.tile([P, PASSES2, PACK], F32)
-        nc.vector.tensor_copy(out=shift[:], in_=shift_raw[:])
 
+        w2_gathered = [None] * UNITS
         for u in range(UNITS):
-            if u + 1 < UNITS:
-                following = quantise_w1(transpose_unit(w1_raw[u + 1], PASSES1))
+            now_gathered = w1_gathered if u + 1 < UNITS else w2_gathered[0]
+            if u + 2 < UNITS:
+                w1_gathered = gather_w1(u + 2)
             else:
-                quantise_w2(0, transpose_unit(w2_raw[0], PASSES2))
+                w2_gathered[u + 2 - UNITS] = gather_w2(u + 2 - UNITS)
+            if u + 1 < UNITS:
+                following = quantise_w1(transpose_unit(w1_raw[u + 1], PASSES1, now_gathered))
+            else:
+                quantise_w2(0, transpose_unit(w2_raw[0], PASSES2, now_gathered))
             if u > 0:
                 statistics(u - 1)
             first_matmul(u, ready[0], ready[1])
@@ -173,12 +204,13 @@ def tile_crossfusion_pa_kernel(
         for i in range(TOKEN_TILES):
             nc.sync.dma_start(out=llm_out[i * P : (i + 1) * P, :], in_=llm[:, i, :])
 
-        w2_grouped = [transpose_unit(w2_raw[u], PASSES2) for u in (1, 2)]
+        w2_grouped = [transpose_unit(w2_raw[1], PASSES2, w2_gathered[1])]
         mean_var = keep.tile([P, TOKEN_TILES, 2], F32)
         for i in range(TOKEN_TILES):
             nc.vector.bn_aggr(out=mean_var[:, i, :], in_=stats[:, i, :, :].rearrange("p u s -> p (u s)"))
         std = keep.tile([P, TOKEN_TILES], F32)
         nc.scalar.activation(out=std[:], in_=mean_var[:, :, 1], func=ACT.Sqrt, bias=eps[:, 0:1], scale=1.0)
+        w2_gathered[2] = gather_w2(2)
         rstd = keep.tile([P, TOKEN_TILES], F32)
         nc.vector.reciprocal(out=rstd[:], in_=std[:])
         offset = keep.tile([P, TOKEN_TILES], F32)
@@ -191,23 +223,18 @@ def tile_crossfusion_pa_kernel(
             for i in range(TOKEN_TILES):
                 source = llm[:, i, g * K_PASS : (g + 1) * K_PASS].rearrange("n (p t) -> n p t", t=PACK)
                 target = xhat[:, i, g, :, :].rearrange("n t p -> n p t")
-                if i == 0:
-                    nc.vector.tensor_scalar(
-                        out=target, in0=source, scalar1=rstd[:, i : i + 1], scalar2=offset[:, i : i + 1],
-                        op0=ALU.mult, op1=ALU.add,
-                    )
-                else:
-                    nc.scalar.activation(
-                        out=target, in_=source, func=ACT.Identity, scale=rstd[:, i : i + 1], bias=offset[:, i : i + 1]
-                    )
+                nc.vector.tensor_scalar(
+                    out=target, in0=source, scalar1=rstd[:, i : i + 1], scalar2=offset[:, i : i + 1],
+                    op0=ALU.mult, op1=ALU.add,
+                )
         quantise_w2(1, w2_grouped[0])
-        quantise_w2(2, w2_grouped[1])
+        w2_grouped.append(transpose_unit(w2_raw[2], PASSES2, w2_gathered[2]))
 
         n_codes = keep.tile([P, PASSES2, TOKENS], U32, align_bytes=64)
         n_scales = keep.tile([P, PASSES2, TOKENS], U8, align_bytes=64)
         n_grouped = []
         for g in range(PASSES2):
-            planes = stage.tile([P, PACK, TOKENS], BF16, tag="planes", name="planes", bufs=2)
+            planes = stage.tile([P, PACK, TOKENS], BF16, tag="planes", name="planes", bufs=3)
             for u in range(2):
                 bank = psum.tile([P, 2, TOKENS], F32, tag="bank", name="bank")
                 for e in range(2):
@@ -215,16 +242,10 @@ def tile_crossfusion_pa_kernel(
                         nc.tensor.transpose(bank[:, e, i * P : (i + 1) * P], xhat[:, i, g, 2 * u + e, :], ident[:])
                 for e in range(2):
                     t = 2 * u + e
-                    if u == 0:
-                        nc.scalar.activation(
-                            out=planes[:, t, :], in_=bank[:, e, :], func=ACT.Identity,
-                            scale=gain[:, g, t : t + 1], bias=shift[:, g, t : t + 1],
-                        )
-                    else:
-                        nc.vector.tensor_scalar(
-                            out=planes[:, t, :], in0=bank[:, e, :], scalar1=gain[:, g, t : t + 1],
-                            scalar2=shift[:, g, t : t + 1], op0=ALU.mult, op1=ALU.add,
-                        )
+                    nc.scalar.activation(
+                        out=planes[:, t, :], in_=bank[:, e, :], func=ACT.Identity,
+                        scale=gain[:, g, t : t + 1], bias=shift[:, g, t : t + 1],
+                    )
             grouped = stage.tile([P, TOKENS * PACK], BF16, align_bytes=64, tag="n_grouped", name="n_grouped", bufs=3)
             nc.vector.tensor_copy(
                 out=grouped[:].rearrange("p (r t) -> p r t", t=PACK), in_=planes[:].rearrange("p t r -> p r t")
@@ -234,14 +255,19 @@ def tile_crossfusion_pa_kernel(
                 nc.vector.quantize_mx(
                     out=n_codes[:, g - 1, :].bitcast(FP8X4), scales=n_scales[:, g - 1, :], in_=n_grouped[g - 1][:]
                 )
+        w2_gathered[3] = gather_w2(3)
         last = PASSES2 - 1
         nc.vector.quantize_mx(out=n_codes[:, last, :].bitcast(FP8X4), scales=n_scales[:, last, :], in_=n_grouped[last][:])
 
-        quantise_w2(3, transpose_unit(w2_raw[3], PASSES2))
+        quantise_w2(2, w2_grouped[1])
+        w2_gathered[4] = gather_w2(4)
+        quantise_w2(3, transpose_unit(w2_raw[3], PASSES2, w2_gathered[3]))
+        w2_gathered[5] = gather_w2(5)
+
         q_sb = keep.tile([P, TOKEN_TILES, DIM], F32)
         for c in range(CHUNKS):
             if c + 4 < UNITS:
-                quantise_w2(c + 4, transpose_unit(w2_raw[c + 4], PASSES2))
+                quantise_w2(c + 4, transpose_unit(w2_raw[c + 4], PASSES2, w2_gathered[c + 4]))
             cols = slice(c * BANK, (c + 1) * BANK)
             for i in range(TOKEN_TILES):
                 tokens = slice(i * P, (i + 1) * P)

@@ -82,33 +82,18 @@ def tile_crossfusion_pa_kernel(
         shift = keep.tile([P, PASSES2, PACK], F32)
         nc.gpsimd.tensor_copy(out=shift[:], in_=shift_raw[:])
 
-        def gather_unit(raw, passes, engines):
-            gathered_tiles = []
-            in_tile = passes // len(raw)
-            for g in range(passes):
-                if engines[g] is None:
-                    gathered_tiles.append(None)
-                    continue
-                first = (g % in_tile) * ROWS
-                words = raw[g // in_tile][:].bitcast(F32)[:, :, first : first + ROWS]
-                gathered = stage.tile([P, 2, 2, P], F32, tag="gathered", name="gathered")
-                engines[g](out=gathered[:], in_=words.rearrange("p r (m u) -> p r u m", u=2))
-                gathered_tiles.append(gathered)
-            return gathered_tiles
-
-        def transpose_unit(raw, passes, gathered_tiles):
+        def transpose_unit(raw, passes):
             grouped_tiles = []
             in_tile = passes // len(raw)
             for g in range(passes):
                 words = raw[g // in_tile][:].bitcast(F32)
                 first = (g % in_tile) * ROWS
-                gathered = gathered_tiles[g]
                 bank = psum.tile([P, 2, ROWS], F32, tag="bank", name="bank")
                 for u in range(2):
                     for r in range(2):
                         nc.tensor.transpose(
                             bank[:, u, r * P : (r + 1) * P],
-                            gathered[:, r, u, :] if gathered is not None else words[:, r, first + u : first + ROWS : 2],
+                            words[:, r, first + u : first + ROWS : 2],
                             ident[:],
                         )
                 grouped = stage.tile([P, ROWS * PACK], BF16, align_bytes=64, tag="grouped", name="grouped")
@@ -168,15 +153,8 @@ def tile_crossfusion_pa_kernel(
             for i in range(TOKEN_TILES):
                 nc.vector.bn_stats(out=stats[:, i, u, :], in_=llm[:, i, u * ROWS : (u + 1) * ROWS])
 
-        def gather_w1(u):
-            return gather_unit(w1_raw[u], PASSES1, (nc.vector.tensor_copy, None, nc.scalar.copy, None))
-
-        def gather_w2(u):
-            return gather_unit(w2_raw[u], PASSES2, ((nc.vector.tensor_copy, None, None), (nc.vector.tensor_copy, None, None), (None, None, None), (None, None, None), (None, None, None), (None, None, None))[u])
-
-        quantise_unit(transpose_unit(x_raw, PASSES1, [None] * PASSES1), x_codes, x_scales, slice(0, TOKENS))
-        ready = quantise_w1(transpose_unit(w1_raw[0], PASSES1, [None] * PASSES1))
-        w1_gathered = gather_w1(1)
+        quantise_unit(transpose_unit(x_raw, PASSES1), x_codes, x_scales, slice(0, TOKENS))
+        ready = quantise_w1(transpose_unit(w1_raw[0], PASSES1))
 
         for c in range(CHUNKS):
             bank = psum.tile([P, BANK], F32, tag="bank", name="bank")
@@ -185,17 +163,11 @@ def tile_crossfusion_pa_kernel(
             )
             nc.vector.tensor_copy(out=b1_all[:, c * BANK : (c + 1) * BANK], in_=bank[:])
 
-        w2_gathered = [None] * UNITS
         for u in range(UNITS):
-            now_gathered = w1_gathered if u + 1 < UNITS else w2_gathered[0]
-            if u + 2 < UNITS:
-                w1_gathered = gather_w1(u + 2)
-            else:
-                w2_gathered[u + 2 - UNITS] = gather_w2(u + 2 - UNITS)
             if u + 1 < UNITS:
-                following = quantise_w1(transpose_unit(w1_raw[u + 1], PASSES1, now_gathered))
+                following = quantise_w1(transpose_unit(w1_raw[u + 1], PASSES1))
             else:
-                quantise_w2(0, transpose_unit(w2_raw[0], PASSES2, now_gathered))
+                quantise_w2(0, transpose_unit(w2_raw[0], PASSES2))
             if u > 0:
                 statistics(u - 1)
             first_matmul(u, ready[0], ready[1])
@@ -204,13 +176,12 @@ def tile_crossfusion_pa_kernel(
         for i in range(TOKEN_TILES):
             nc.sync.dma_start(out=llm_out[i * P : (i + 1) * P, :], in_=llm[:, i, :])
 
-        w2_grouped = [transpose_unit(w2_raw[1], PASSES2, w2_gathered[1])]
+        w2_grouped = [transpose_unit(w2_raw[1], PASSES2)]
         mean_var = keep.tile([P, TOKEN_TILES, 2], F32)
         for i in range(TOKEN_TILES):
             nc.vector.bn_aggr(out=mean_var[:, i, :], in_=stats[:, i, :, :].rearrange("p u s -> p (u s)"))
         std = keep.tile([P, TOKEN_TILES], F32)
         nc.scalar.activation(out=std[:], in_=mean_var[:, :, 1], func=ACT.Sqrt, bias=eps[:, 0:1], scale=1.0)
-        w2_gathered[2] = gather_w2(2)
         rstd = keep.tile([P, TOKEN_TILES], F32)
         nc.vector.reciprocal(out=rstd[:], in_=std[:])
         offset = keep.tile([P, TOKEN_TILES], F32)
@@ -228,7 +199,7 @@ def tile_crossfusion_pa_kernel(
                     op0=ALU.mult, op1=ALU.add,
                 )
         quantise_w2(1, w2_grouped[0])
-        w2_grouped.append(transpose_unit(w2_raw[2], PASSES2, w2_gathered[2]))
+        w2_grouped.append(transpose_unit(w2_raw[2], PASSES2))
 
         n_codes = keep.tile([P, PASSES2, TOKENS], U32, align_bytes=64)
         n_scales = keep.tile([P, PASSES2, TOKENS], U8, align_bytes=64)
@@ -255,19 +226,16 @@ def tile_crossfusion_pa_kernel(
                 nc.vector.quantize_mx(
                     out=n_codes[:, g - 1, :].bitcast(FP8X4), scales=n_scales[:, g - 1, :], in_=n_grouped[g - 1][:]
                 )
-        w2_gathered[3] = gather_w2(3)
         last = PASSES2 - 1
         nc.vector.quantize_mx(out=n_codes[:, last, :].bitcast(FP8X4), scales=n_scales[:, last, :], in_=n_grouped[last][:])
 
         quantise_w2(2, w2_grouped[1])
-        w2_gathered[4] = gather_w2(4)
-        quantise_w2(3, transpose_unit(w2_raw[3], PASSES2, w2_gathered[3]))
-        w2_gathered[5] = gather_w2(5)
+        quantise_w2(3, transpose_unit(w2_raw[3], PASSES2))
 
         q_sb = keep.tile([P, TOKEN_TILES, DIM], F32)
         for c in range(CHUNKS):
             if c + 4 < UNITS:
-                quantise_w2(c + 4, transpose_unit(w2_raw[c + 4], PASSES2, w2_gathered[c + 4]))
+                quantise_w2(c + 4, transpose_unit(w2_raw[c + 4], PASSES2))
             cols = slice(c * BANK, (c + 1) * BANK)
             for i in range(TOKEN_TILES):
                 tokens = slice(i * P, (i + 1) * P)

@@ -76,26 +76,40 @@ def tile_crossfusion_pa_kernel(
         eps = keep.tile([P, 1], F32)
         nc.vector.memset(eps[:], EPS)
         warm = keep.tile([P, 1], F32)
-        nc.scalar.activation(out=warm[:], in_=eps[:], func=ACT.Sqrt)
+        nc.scalar.activation(out=warm[:], in_=eps[:], func=ACT.Abs_reciprocal_sqrt)
         gain = keep.tile([P, PASSES2, PACK], F32)
         nc.gpsimd.tensor_copy(out=gain[:], in_=gain_raw[:])
         shift = keep.tile([P, PASSES2, PACK], F32)
         nc.gpsimd.tensor_copy(out=shift[:], in_=shift_raw[:])
 
-        def transpose_unit(raw, passes):
+        def gather_unit(raw, passes, copies):
+            in_tile = passes // len(raw)
+            gathered_tiles = []
+            for g in range(passes):
+                gathered_tiles.append(None)
+                if copies[g] is not None:
+                    first = (g % in_tile) * ROWS
+                    words = raw[g // in_tile][:].bitcast(F32)[:, :, first : first + ROWS]
+                    gathered = stage.tile([P, 2, 2, P], F32, tag="gathered", name="gathered")
+                    copies[g](out=gathered[:], in_=words.rearrange("p r (m u) -> p r u m", u=2))
+                    gathered_tiles[g] = gathered
+            return gathered_tiles
+
+        def transpose_unit(raw, passes, gathered_tiles=None):
             grouped_tiles = []
             in_tile = passes // len(raw)
             for g in range(passes):
                 words = raw[g // in_tile][:].bitcast(F32)
                 first = (g % in_tile) * ROWS
+                gathered = None if gathered_tiles is None else gathered_tiles[g]
                 bank = psum.tile([P, 2, ROWS], F32, tag="bank", name="bank")
                 for u in range(2):
                     for r in range(2):
-                        nc.tensor.transpose(
-                            bank[:, u, r * P : (r + 1) * P],
-                            words[:, r, first + u : first + ROWS : 2],
-                            ident[:],
-                        )
+                        if gathered is None:
+                            run = words[:, r, first + u : first + ROWS : 2]
+                        else:
+                            run = gathered[:, r, u, :]
+                        nc.tensor.transpose(bank[:, u, r * P : (r + 1) * P], run, ident[:])
                 grouped = stage.tile([P, ROWS * PACK], BF16, align_bytes=64, tag="grouped", name="grouped")
                 nc.scalar.copy(
                     out=grouped[:].bitcast(F32).rearrange("p (c u) -> p c u", u=2),
@@ -153,6 +167,8 @@ def tile_crossfusion_pa_kernel(
             for i in range(TOKEN_TILES):
                 nc.vector.bn_stats(out=stats[:, i, u, :], in_=llm[:, i, u * ROWS : (u + 1) * ROWS])
 
+        w1_copies = (None, None, nc.vector.tensor_copy, nc.scalar.copy)
+
         quantise_unit(transpose_unit(x_raw, PASSES1), x_codes, x_scales, slice(0, TOKENS))
         ready = quantise_w1(transpose_unit(w1_raw[0], PASSES1))
 
@@ -163,11 +179,14 @@ def tile_crossfusion_pa_kernel(
             )
             nc.vector.tensor_copy(out=b1_all[:, c * BANK : (c + 1) * BANK], in_=bank[:])
 
+        w1_gathered = None
         for u in range(UNITS):
             if u + 1 < UNITS:
-                following = quantise_w1(transpose_unit(w1_raw[u + 1], PASSES1))
+                following = quantise_w1(transpose_unit(w1_raw[u + 1], PASSES1, w1_gathered))
             else:
                 quantise_w2(0, transpose_unit(w2_raw[0], PASSES2))
+            if u + 2 < UNITS:
+                w1_gathered = gather_unit(w1_raw[u + 2], PASSES1, w1_copies)
             if u > 0:
                 statistics(u - 1)
             first_matmul(u, ready[0], ready[1])
@@ -180,13 +199,9 @@ def tile_crossfusion_pa_kernel(
         mean_var = keep.tile([P, TOKEN_TILES, 2], F32)
         for i in range(TOKEN_TILES):
             nc.vector.bn_aggr(out=mean_var[:, i, :], in_=stats[:, i, :, :].rearrange("p u s -> p (u s)"))
-        std = keep.tile([P, TOKEN_TILES], F32)
-        nc.scalar.activation(out=std[:], in_=mean_var[:, :, 1], func=ACT.Sqrt, bias=eps[:, 0:1], scale=1.0)
         rstd = keep.tile([P, TOKEN_TILES], F32)
-        nc.vector.reciprocal(out=rstd[:], in_=std[:])
-        offset = keep.tile([P, TOKEN_TILES], F32)
-        nc.vector.scalar_tensor_tensor(
-            out=offset[:], in0=mean_var[:, :, 0], scalar=-1.0, in1=rstd[:], op0=ALU.mult, op1=ALU.mult
+        nc.scalar.activation(
+            out=rstd[:], in_=mean_var[:, :, 1], func=ACT.Abs_reciprocal_sqrt, bias=eps[:, 0:1], scale=1.0
         )
 
         xhat = keep.tile([P, TOKEN_TILES, PASSES2, PACK, P], F32)
@@ -195,8 +210,8 @@ def tile_crossfusion_pa_kernel(
                 source = llm[:, i, g * K_PASS : (g + 1) * K_PASS].rearrange("n (p t) -> n p t", t=PACK)
                 target = xhat[:, i, g, :, :].rearrange("n t p -> n p t")
                 nc.vector.tensor_scalar(
-                    out=target, in0=source, scalar1=rstd[:, i : i + 1], scalar2=offset[:, i : i + 1],
-                    op0=ALU.mult, op1=ALU.add,
+                    out=target, in0=source, scalar1=mean_var[:, i, 0:1], scalar2=rstd[:, i : i + 1],
+                    op0=ALU.subtract, op1=ALU.mult,
                 )
         quantise_w2(1, w2_grouped[0])
         w2_grouped.append(transpose_unit(w2_raw[2], PASSES2))

@@ -24,6 +24,8 @@ UNITS = DIM // ROWS
 BANK = 512
 CHUNKS = DIM // BANK
 EPS = 1e-5
+B1_PIECES = 4
+B1_PIECE = DIM // B1_PIECES
 
 FLOPS = 2 * TOKENS * K1 * DIM + 2 * TOKENS * DIM * DIM
 
@@ -54,25 +56,25 @@ def tile_crossfusion_pa_kernel(
             return pieces
 
         x_raw = load_unit(x_rows, K1, "x_raw", 2)
-        ones = keep.tile([P, P], BF16)
-        nc.vector.memset(ones[:], 1.0)
-        b1_rows = keep.tile([P, DIM], BF16)
+        b1_rows = keep.tile([P, B1_PIECE], BF16)
         nc.vector.memset(b1_rows[:].bitcast(I32), 0)
-        nc.scalar.dma_start(out=b1_rows[0:1, :], in_=llm_proj_b.rearrange("(o n) -> o n", o=1))
-        gain_raw = keep.tile([P, PASSES2, PACK], BF16)
-        nc.scalar.dma_start(out=gain_raw[:], in_=kvn_g.rearrange("(g p t) -> p g t", p=P, t=PACK))
-        shift_raw = keep.tile([P, PASSES2, PACK], BF16)
-        nc.scalar.dma_start(out=shift_raw[:], in_=kvn_b.rearrange("(g p t) -> p g t", p=P, t=PACK))
+        nc.scalar.dma_start(out=b1_rows[0:B1_PIECES, :], in_=llm_proj_b.rearrange("(c n) -> c n", n=B1_PIECE))
         w1_raw = [
             load_unit(llm_proj_w[u * ROWS : (u + 1) * ROWS, :], K1, "w1_raw%d" % u, 2 if u < 2 else 1)
             for u in range(UNITS)
         ]
+        gain_raw = keep.tile([P, PASSES2, PACK], BF16)
+        nc.sync.dma_start(out=gain_raw[:], in_=kvn_g.rearrange("(g p t) -> p g t", p=P, t=PACK))
+        shift_raw = keep.tile([P, PASSES2, PACK], BF16)
+        nc.sync.dma_start(out=shift_raw[:], in_=kvn_b.rearrange("(g p t) -> p g t", p=P, t=PACK))
         w2_raw = [load_unit(q_w[u * ROWS : (u + 1) * ROWS, :], DIM, "w2_raw%d" % u) for u in range(UNITS)]
         qb_all = keep.tile([P, DIM], BF16)
         nc.sync.dma_start(out=qb_all[:], in_=q_b.partition_broadcast(P))
 
         ident = keep.tile([P, P], F32)
         make_identity(nc, ident[:])
+        select = keep.tile([P, B1_PIECES], BF16)
+        nc.gpsimd.tensor_copy(out=select[:], in_=ident[:, 0:B1_PIECES])
         eps = keep.tile([P, 1], F32)
         nc.vector.memset(eps[:], EPS)
         warm = keep.tile([P, 1], F32)
@@ -168,25 +170,30 @@ def tile_crossfusion_pa_kernel(
                 nc.vector.bn_stats(out=stats[:, i, u, :], in_=llm[:, i, u * ROWS : (u + 1) * ROWS])
 
         w1_copies = (None, None, nc.vector.tensor_copy, nc.scalar.copy)
+        w2_copies = (None, None, nc.vector.tensor_copy)
 
         quantise_unit(transpose_unit(x_raw, PASSES1), x_codes, x_scales, slice(0, TOKENS))
         ready = quantise_w1(transpose_unit(w1_raw[0], PASSES1))
 
-        for c in range(CHUNKS):
+        for c in range(B1_PIECES):
             bank = psum.tile([P, BANK], F32, tag="bank", name="bank")
             nc.tensor.matmul(
-                out=bank[:], lhsT=ones[:], rhs=b1_rows[:, c * BANK : (c + 1) * BANK], start=True, stop=True
+                out=bank[:, 0:B1_PIECE], lhsT=select[:, c : c + 1].to_broadcast([P, P]), rhs=b1_rows[:], start=True, stop=True
             )
-            nc.vector.tensor_copy(out=b1_all[:, c * BANK : (c + 1) * BANK], in_=bank[:])
+            nc.vector.tensor_copy(out=b1_all[:, c * B1_PIECE : (c + 1) * B1_PIECE], in_=bank[:, 0:B1_PIECE])
 
         w1_gathered = None
+        w2_gathered = [None] * UNITS
         for u in range(UNITS):
             if u + 1 < UNITS:
                 following = quantise_w1(transpose_unit(w1_raw[u + 1], PASSES1, w1_gathered))
             else:
-                quantise_w2(0, transpose_unit(w2_raw[0], PASSES2))
+                w2_grouped = [transpose_unit(w2_raw[0], PASSES2, w2_gathered[0])]
             if u + 2 < UNITS:
                 w1_gathered = gather_unit(w1_raw[u + 2], PASSES1, w1_copies)
+            elif u + 1 < UNITS:
+                for v in range(2):
+                    w2_gathered[v] = gather_unit(w2_raw[v], PASSES2, w2_copies)
             if u > 0:
                 statistics(u - 1)
             first_matmul(u, ready[0], ready[1])
@@ -195,10 +202,11 @@ def tile_crossfusion_pa_kernel(
         for i in range(TOKEN_TILES):
             nc.sync.dma_start(out=llm_out[i * P : (i + 1) * P, :], in_=llm[:, i, :])
 
-        w2_grouped = [transpose_unit(w2_raw[1], PASSES2)]
+        w2_grouped.append(transpose_unit(w2_raw[1], PASSES2, w2_gathered[1]))
         mean_var = keep.tile([P, TOKEN_TILES, 2], F32)
         for i in range(TOKEN_TILES):
             nc.vector.bn_aggr(out=mean_var[:, i, :], in_=stats[:, i, :, :].rearrange("p u s -> p (u s)"))
+        quantise_w2(0, w2_grouped[0])
         rstd = keep.tile([P, TOKEN_TILES], F32)
         nc.scalar.activation(
             out=rstd[:], in_=mean_var[:, :, 1], func=ACT.Abs_reciprocal_sqrt, bias=eps[:, 0:1], scale=1.0
@@ -213,8 +221,10 @@ def tile_crossfusion_pa_kernel(
                     out=target, in0=source, scalar1=mean_var[:, i, 0:1], scalar2=rstd[:, i : i + 1],
                     op0=ALU.subtract, op1=ALU.mult,
                 )
-        quantise_w2(1, w2_grouped[0])
-        w2_grouped.append(transpose_unit(w2_raw[2], PASSES2))
+        w2_gathered[3] = gather_unit(w2_raw[3], PASSES2, w2_copies)
+        w2_grouped.append(transpose_unit(w2_raw[2], PASSES2, w2_gathered[2]))
+        for v in range(1, 3):
+            quantise_w2(v, w2_grouped[v])
 
         n_codes = keep.tile([P, PASSES2, TOKENS], U32, align_bytes=64)
         n_scales = keep.tile([P, PASSES2, TOKENS], U8, align_bytes=64)
@@ -244,26 +254,34 @@ def tile_crossfusion_pa_kernel(
         last = PASSES2 - 1
         nc.vector.quantize_mx(out=n_codes[:, last, :].bitcast(FP8X4), scales=n_scales[:, last, :], in_=n_grouped[last][:])
 
-        quantise_w2(2, w2_grouped[1])
-        quantise_w2(3, transpose_unit(w2_raw[3], PASSES2))
+        quantise_w2(3, transpose_unit(w2_raw[3], PASSES2, w2_gathered[3]))
+
+        quantise_w2(4, transpose_unit(w2_raw[4], PASSES2, w2_gathered[4]))
+        last_unit = transpose_unit(w2_raw[5], PASSES2, w2_gathered[5])
 
         q_sb = keep.tile([P, TOKEN_TILES, DIM], F32)
+
+        def second_matmul(i, cols):
+            tokens = slice(i * P, (i + 1) * P)
+            bank = psum.tile([P, BANK], F32, tag="bank", name="acc")
+            acc = bank[:, 0 : cols.stop - cols.start]
+            for g in range(PASSES2):
+                nc.tensor.matmul_mx(
+                    out=acc,
+                    lhsT=n_codes[:, g, tokens].bitcast(FP8X4),
+                    lhsT_scale=n_scales[:, g, tokens],
+                    rhs=w2_codes[:, g, cols].bitcast(FP8X4),
+                    rhs_scale=w2_scales[:, g, cols],
+                    start=(g == 0),
+                    stop=(g == PASSES2 - 1),
+                )
+            nc.vector.tensor_tensor(out=q_sb[:, i, cols], in0=acc, in1=qb_all[:, cols], op=ALU.add)
+            nc.sync.dma_start(out=q_out[i * P : (i + 1) * P, cols], in_=q_sb[:, i, cols])
+
         for c in range(CHUNKS):
-            if c + 4 < UNITS:
-                quantise_w2(c + 4, transpose_unit(w2_raw[c + 4], PASSES2))
-            cols = slice(c * BANK, (c + 1) * BANK)
+            if c == 1:
+                quantise_w2(UNITS - 1, last_unit)
             for i in range(TOKEN_TILES):
-                tokens = slice(i * P, (i + 1) * P)
-                acc = psum.tile([P, BANK], F32, tag="bank", name="acc")
-                for g in range(PASSES2):
-                    nc.tensor.matmul_mx(
-                        out=acc[:],
-                        lhsT=n_codes[:, g, tokens].bitcast(FP8X4),
-                        lhsT_scale=n_scales[:, g, tokens],
-                        rhs=w2_codes[:, g, cols].bitcast(FP8X4),
-                        rhs_scale=w2_scales[:, g, cols],
-                        start=(g == 0),
-                        stop=(g == PASSES2 - 1),
-                    )
-                nc.vector.tensor_tensor(out=q_sb[:, i, cols], in0=acc[:], in1=qb_all[:, cols], op=ALU.add)
-                nc.sync.dma_start(out=q_out[i * P : (i + 1) * P, cols], in_=q_sb[:, i, cols])
+                width = ROWS if c == CHUNKS - 1 and i == TOKEN_TILES - 1 else BANK
+                for first in range(c * BANK, (c + 1) * BANK, width):
+                    second_matmul(i, slice(first, first + width))

@@ -35,8 +35,8 @@ def tile_crossfusion_pa_kernel(
 ):
     nc = tc.nc
     x_rows = llm_embed.flatten_outer_dims()
-    llm_out = out_0.flatten_outer_dims()
-    q_out = out_1.flatten_outer_dims()
+    llm_out = out_0.flatten_outer_dims().rearrange("(p i) n -> p i n", i=TOKEN_TILES)
+    q_out = out_1.flatten_outer_dims().rearrange("(p i) n -> p i n", i=TOKEN_TILES)
 
     with tc.tile_pool(name="keep", bufs=1) as keep, tc.tile_pool(
         name="stage", bufs=8
@@ -45,13 +45,12 @@ def tile_crossfusion_pa_kernel(
     ) as psum, tc.manual_schedule():
 
         def load_unit(rows, width, name, parts=1):
+            rows = rows.rearrange("(p r) k -> p r k", r=2)
             pieces = []
             step = width // parts
             for c in range(parts):
                 raw = keep.tile([P, 2, step], BF16, name="%s_%d" % (name, c))
-                nc.sync.dma_start(
-                    out=raw[:], in_=rows[:, c * step : (c + 1) * step].rearrange("(r p) k -> p r k", p=P)
-                )
+                nc.sync.dma_start(out=raw[:], in_=rows[:, :, c * step : (c + 1) * step])
                 pieces.append(raw)
             return pieces
 
@@ -97,10 +96,10 @@ def tile_crossfusion_pa_kernel(
                     gathered_tiles[g] = gathered
             return gathered_tiles
 
-        def transpose_unit(raw, passes, gathered_tiles=None):
+        def transpose_unit(raw, passes, gathered_tiles=None, only=slice(None)):
             grouped_tiles = []
             in_tile = passes // len(raw)
-            for g in range(passes):
+            for g in range(passes)[only]:
                 words = raw[g // in_tile][:].bitcast(F32)
                 first = (g % in_tile) * ROWS
                 gathered = None if gathered_tiles is None else gathered_tiles[g]
@@ -120,8 +119,8 @@ def tile_crossfusion_pa_kernel(
                 grouped_tiles.append(grouped)
             return grouped_tiles
 
-        def quantise_unit(grouped_tiles, codes, scales, cols):
-            for g, grouped in enumerate(grouped_tiles):
+        def quantise_unit(grouped_tiles, codes, scales, cols, first_pass=0):
+            for g, grouped in enumerate(grouped_tiles, first_pass):
                 nc.vector.quantize_mx(
                     out=codes[:, g, cols].bitcast(FP8X4), scales=scales[:, g, cols], in_=grouped[:]
                 )
@@ -159,9 +158,12 @@ def tile_crossfusion_pa_kernel(
                     )
             cols = slice(u * ROWS, (u + 1) * ROWS)
             nc.vector.tensor_tensor(
-                out=llm[:, :, cols],
-                in0=acc[:],
-                in1=b1_all[:, cols].unsqueeze(1).to_broadcast([P, TOKEN_TILES, ROWS]),
+                out=llm[:, :, cols].rearrange("p i (m r) -> p i m r", r=2),
+                in0=acc[:].rearrange("p i (r m) -> p i m r", r=2),
+                in1=b1_all[:, cols]
+                .rearrange("p (m r) -> p m r", r=2)
+                .unsqueeze(1)
+                .to_broadcast([P, TOKEN_TILES, P, 2]),
                 op=ALU.add,
             )
 
@@ -200,17 +202,18 @@ def tile_crossfusion_pa_kernel(
             ready = following
         statistics(UNITS - 1)
         for i in range(TOKEN_TILES):
-            nc.sync.dma_start(out=llm_out[i * P : (i + 1) * P, :], in_=llm[:, i, :])
+            nc.sync.dma_start(out=llm_out[:, i, :], in_=llm[:, i, :])
 
-        w2_grouped.append(transpose_unit(w2_raw[1], PASSES2, w2_gathered[1]))
+        w2_grouped.append(transpose_unit(w2_raw[1], PASSES2, w2_gathered[1], slice(0, 2)))
         mean_var = keep.tile([P, TOKEN_TILES, 2], F32)
         for i in range(TOKEN_TILES):
             nc.vector.bn_aggr(out=mean_var[:, i, :], in_=stats[:, i, :, :].rearrange("p u s -> p (u s)"))
-        quantise_w2(0, w2_grouped[0])
+        quantise_unit(w2_grouped[0][0:1], w2_codes, w2_scales, slice(0, ROWS))
         rstd = keep.tile([P, TOKEN_TILES], F32)
         nc.scalar.activation(
             out=rstd[:], in_=mean_var[:, :, 1], func=ACT.Abs_reciprocal_sqrt, bias=eps[:, 0:1], scale=1.0
         )
+        w2_grouped[1].extend(transpose_unit(w2_raw[1], PASSES2, w2_gathered[1], slice(2, PASSES2)))
 
         xhat = keep.tile([P, TOKEN_TILES, PASSES2, PACK, P], F32)
         for g in range(PASSES2):
@@ -223,6 +226,7 @@ def tile_crossfusion_pa_kernel(
                 )
         w2_gathered[3] = gather_unit(w2_raw[3], PASSES2, w2_copies)
         w2_grouped.append(transpose_unit(w2_raw[2], PASSES2, w2_gathered[2]))
+        quantise_unit(w2_grouped[0][1:3], w2_codes, w2_scales, slice(0, ROWS), 1)
         for v in range(1, 3):
             quantise_w2(v, w2_grouped[v])
 
@@ -275,8 +279,13 @@ def tile_crossfusion_pa_kernel(
                     start=(g == 0),
                     stop=(g == PASSES2 - 1),
                 )
-            nc.vector.tensor_tensor(out=q_sb[:, i, cols], in0=acc, in1=qb_all[:, cols], op=ALU.add)
-            nc.sync.dma_start(out=q_out[i * P : (i + 1) * P, cols], in_=q_sb[:, i, cols])
+            nc.vector.tensor_tensor(
+                out=q_sb[:, i, cols].rearrange("p (v m r) -> p v m r", m=P, r=2),
+                in0=acc.rearrange("p (v r m) -> p v m r", m=P, r=2),
+                in1=qb_all[:, cols].rearrange("p (v m r) -> p v m r", m=P, r=2),
+                op=ALU.add,
+            )
+            nc.sync.dma_start(out=q_out[:, i, cols], in_=q_sb[:, i, cols])
 
         for c in range(CHUNKS):
             if c == 1:

@@ -130,7 +130,7 @@ def tile_crossfusion_pa_kernel(
         w2_codes = keep.tile([P, PASSES2, DIM], U32, align_bytes=64)
         w2_scales = keep.tile([P, PASSES2, DIM], U8, align_bytes=64)
         b1_all = keep.tile([P, DIM], BF16)
-        llm = keep.tile([P, TOKEN_TILES, DIM], F32)
+        llm = keep.tile([P, UNITS, TOKEN_TILES, ROWS], F32)
         stats = keep.tile([P, TOKEN_TILES, UNITS, 6], F32)
 
         def quantise_w1(grouped_tiles):
@@ -158,7 +158,7 @@ def tile_crossfusion_pa_kernel(
                     )
             cols = slice(u * ROWS, (u + 1) * ROWS)
             nc.vector.tensor_tensor(
-                out=llm[:, :, cols].rearrange("p i (m r) -> p i m r", r=2),
+                out=llm[:, u, :, :].rearrange("p i (m r) -> p i m r", r=2),
                 in0=acc[:].rearrange("p i (r m) -> p i m r", r=2),
                 in1=b1_all[:, cols]
                 .rearrange("p (m r) -> p m r", r=2)
@@ -169,9 +169,10 @@ def tile_crossfusion_pa_kernel(
 
         def statistics(u):
             for i in range(TOKEN_TILES):
-                nc.vector.bn_stats(out=stats[:, i, u, :], in_=llm[:, i, u * ROWS : (u + 1) * ROWS])
+                nc.vector.bn_stats(out=stats[:, i, u, :], in_=llm[:, u, i, :])
 
         w1_copies = (None, None, nc.vector.tensor_copy, nc.scalar.copy)
+        first_copies = (None, None, None, nc.scalar.copy)
         w2_copies = (None, None, nc.vector.tensor_copy)
 
         quantise_unit(transpose_unit(x_raw, PASSES1), x_codes, x_scales, slice(0, TOKENS))
@@ -192,7 +193,7 @@ def tile_crossfusion_pa_kernel(
             else:
                 w2_grouped = [transpose_unit(w2_raw[0], PASSES2, w2_gathered[0])]
             if u + 2 < UNITS:
-                w1_gathered = gather_unit(w1_raw[u + 2], PASSES1, w1_copies)
+                w1_gathered = gather_unit(w1_raw[u + 2], PASSES1, w1_copies if u > 0 else first_copies)
             elif u + 1 < UNITS:
                 for v in range(2):
                     w2_gathered[v] = gather_unit(w2_raw[v], PASSES2, w2_copies)
@@ -202,7 +203,7 @@ def tile_crossfusion_pa_kernel(
             ready = following
         statistics(UNITS - 1)
         for i in range(TOKEN_TILES):
-            nc.sync.dma_start(out=llm_out[:, i, :], in_=llm[:, i, :])
+            nc.sync.dma_start(out=llm_out[:, i, :].rearrange("p (u c) -> p u c", c=ROWS), in_=llm[:, :, i, :])
 
         w2_grouped.append(transpose_unit(w2_raw[1], PASSES2, w2_gathered[1], slice(0, 2)))
         mean_var = keep.tile([P, TOKEN_TILES, 2], F32)
@@ -218,8 +219,8 @@ def tile_crossfusion_pa_kernel(
         xhat = keep.tile([P, TOKEN_TILES, PASSES2, PACK, P], F32)
         for g in range(PASSES2):
             for i in range(TOKEN_TILES):
-                source = llm[:, i, g * K_PASS : (g + 1) * K_PASS].rearrange("n (p t) -> n p t", t=PACK)
-                target = xhat[:, i, g, :, :].rearrange("n t p -> n p t")
+                source = llm[:, 2 * g : 2 * g + 2, i, :].rearrange("n v (p t) -> n v p t", t=PACK)
+                target = xhat[:, i, g, :, :].rearrange("n t (v p) -> n v p t", v=2)
                 nc.vector.tensor_scalar(
                     out=target, in0=source, scalar1=mean_var[:, i, 0:1], scalar2=rstd[:, i : i + 1],
                     op0=ALU.subtract, op1=ALU.mult,

import concourse.mybir as mybir
from concourse.masks import make_identity

F32 = mybir.dt.float32
BF16 = mybir.dt.bfloat16
U32 = mybir.dt.uint32
U8 = mybir.dt.uint8
I32 = mybir.dt.int32
FP8X4 = mybir.dt.float8_e4m3fn_x4
ALU = mybir.AluOpType
ACT = mybir.ActivationFunctionType

P = 128
PACK = 4
K_PASS = P * PACK
ROWS = 2 * P
TOKENS = 256
TOKEN_TILES = TOKENS // P
K1 = 2048
DIM = 1536
PASSES1 = K1 // K_PASS
PASSES2 = DIM // K_PASS
UNITS = DIM // ROWS
BANK = 512
CHUNKS = DIM // BANK
EPS = 1e-5
B1_PIECES = 4
B1_PIECE = DIM // B1_PIECES

FLOPS = 2 * TOKENS * K1 * DIM + 2 * TOKENS * DIM * DIM


def tile_crossfusion_pa_kernel(
    tc, llm_embed, llm_proj_w, llm_proj_b, kvn_g, kvn_b, q_w, q_b, out_0, out_1
):
    nc = tc.nc
    x_rows = llm_embed.flatten_outer_dims()
    llm_out = out_0.flatten_outer_dims().rearrange("(p i) n -> p i n", i=TOKEN_TILES)
    q_out = out_1.flatten_outer_dims().rearrange("(p i) n -> p i n", i=TOKEN_TILES)

    with tc.tile_pool(name="keep", bufs=1) as keep, tc.tile_pool(
        name="stage", bufs=8
    ) as stage, tc.tile_pool(name="w1q", bufs=3) as w1q, tc.psum_pool(
        name="psum", bufs=8
    ) as psum, tc.manual_schedule():

        def load_unit(rows, width, name, parts=1):
            rows = rows.rearrange("(p r) k -> p r k", r=2)
            pieces = []
            step = width // parts
            for c in range(parts):
                raw = keep.tile([P, 2, step], BF16, name="%s_%d" % (name, c))
                nc.sync.dma_start(out=raw[:], in_=rows[:, :, c * step : (c + 1) * step])
                pieces.append(raw)
            return pieces

        x_raw = load_unit(x_rows, K1, "x_raw", 2)
        b1_rows = keep.tile([P, B1_PIECE], BF16)
        nc.vector.memset(b1_rows[:].bitcast(I32), 0)
        nc.scalar.dma_start(out=b1_rows[0:B1_PIECES, :], in_=llm_proj_b.rearrange("(c n) -> c n", n=B1_PIECE))
        w1_raw = [
            load_unit(llm_proj_w[u * ROWS : (u + 1) * ROWS, :], K1, "w1_raw%d" % u, 2 if u < 2 else 1)
            for u in range(UNITS)
        ]
        gain_raw = keep.tile([P, PASSES2, PACK], BF16)
        nc.sync.dma_start(out=gain_raw[:], in_=kvn_g.rearrange("(g p t) -> p g t", p=P, t=PACK))
        shift_raw = keep.tile([P, PASSES2, PACK], BF16)
        nc.sync.dma_start(out=shift_raw[:], in_=kvn_b.rearrange("(g p t) -> p g t", p=P, t=PACK))
        w2_raw = [load_unit(q_w[u * ROWS : (u + 1) * ROWS, :], DIM, "w2_raw%d" % u) for u in range(UNITS)]
        qb_all = keep.tile([P, DIM], BF16)
        nc.sync.dma_start(out=qb_all[:], in_=q_b.partition_broadcast(P))

        ident = keep.tile([P, P], F32)
        make_identity(nc, ident[:])
        select = keep.tile([P, B1_PIECES], BF16)
        nc.gpsimd.tensor_copy(out=select[:], in_=ident[:, 0:B1_PIECES])
        eps = keep.tile([P, 1], F32)
        nc.vector.memset(eps[:], EPS)
        warm = keep.tile([P, 1], F32)
        nc.scalar.activation(out=warm[:], in_=eps[:], func=ACT.Abs_reciprocal_sqrt)
        gain = keep.tile([P, PASSES2, PACK], F32)
        nc.gpsimd.tensor_copy(out=gain[:], in_=gain_raw[:])
        shift = keep.tile([P, PASSES2, PACK], F32)
        nc.gpsimd.tensor_copy(out=shift[:], in_=shift_raw[:])

        def gather_unit(raw, passes, copies):
            in_tile = passes // len(raw)
            gathered_tiles = []
            for g in range(passes):
                gathered_tiles.append(None)
                if copies[g] is not None:
                    first = (g % in_tile) * ROWS
                    words = raw[g // in_tile][:].bitcast(F32)[:, :, first : first + ROWS]
                    gathered = stage.tile([P, 2, 2, P], F32, tag="gathered", name="gathered")
                    copies[g](out=gathered[:], in_=words.rearrange("p r (m u) -> p r u m", u=2))
                    gathered_tiles[g] = gathered
            return gathered_tiles

        def transpose_unit(raw, passes, gathered_tiles=None, only=slice(None)):
            grouped_tiles = []
            in_tile = passes // len(raw)
            for g in range(passes)[only]:
                words = raw[g // in_tile][:].bitcast(F32)
                first = (g % in_tile) * ROWS
                gathered = None if gathered_tiles is None else gathered_tiles[g]
                bank = psum.tile([P, 2, ROWS], F32, tag="bank", name="bank")
                for u in range(2):
                    for r in range(2):
                        if gathered is None:
                            run = words[:, r, first + u : first + ROWS : 2]
                        else:
                            run = gathered[:, r, u, :]
                        nc.tensor.transpose(bank[:, u, r * P : (r + 1) * P], run, ident[:])
                grouped = stage.tile([P, ROWS * PACK], BF16, align_bytes=64, tag="grouped", name="grouped")
                nc.scalar.copy(
                    out=grouped[:].bitcast(F32).rearrange("p (c u) -> p c u", u=2),
                    in_=bank[:].rearrange("p u c -> p c u"),
                )
                grouped_tiles.append(grouped)
            return grouped_tiles

        def quantise_unit(grouped_tiles, codes, scales, cols, first_pass=0):
            for g, grouped in enumerate(grouped_tiles, first_pass):
                nc.vector.quantize_mx(
                    out=codes[:, g, cols].bitcast(FP8X4), scales=scales[:, g, cols], in_=grouped[:]
                )

        x_codes = keep.tile([P, PASSES1, TOKENS], U32, align_bytes=64)
        x_scales = keep.tile([P, PASSES1, TOKENS], U8, align_bytes=64)
        w2_codes = keep.tile([P, PASSES2, DIM], U32, align_bytes=64)
        w2_scales = keep.tile([P, PASSES2, DIM], U8, align_bytes=64)
        b1_all = keep.tile([P, DIM], BF16)
        llm = keep.tile([P, UNITS, TOKEN_TILES, ROWS], F32)
        stats = keep.tile([P, TOKEN_TILES, UNITS, 6], F32)

        def quantise_w1(grouped_tiles):
            w1_codes = w1q.tile([P, PASSES1, ROWS], U32, align_bytes=64, name="w1_codes")
            w1_scales = w1q.tile([P, PASSES1, ROWS], U8, align_bytes=64, name="w1_scales")
            quantise_unit(grouped_tiles, w1_codes, w1_scales, slice(0, ROWS))
            return w1_codes, w1_scales

        def quantise_w2(u, grouped_tiles):
            quantise_unit(grouped_tiles, w2_codes, w2_scales, slice(u * ROWS, (u + 1) * ROWS))

        def first_matmul(u, w1_codes, w1_scales):
            acc = psum.tile([P, TOKEN_TILES, ROWS], F32, tag="bank", name="acc")
            for i in range(TOKEN_TILES):
                tokens = slice(i * P, (i + 1) * P)
                for g in range(PASSES1):
                    nc.tensor.matmul_mx(
                        out=acc[:, i, :],
                        lhsT=x_codes[:, g, tokens].bitcast(FP8X4),
                        lhsT_scale=x_scales[:, g, tokens],
                        rhs=w1_codes[:, g, :].bitcast(FP8X4),
                        rhs_scale=w1_scales[:, g, :],
                        start=(g == 0),
                        stop=(g == PASSES1 - 1),
                    )
            cols = slice(u * ROWS, (u + 1) * ROWS)
            nc.vector.tensor_tensor(
                out=llm[:, u, :, :].rearrange("p i (m r) -> p i m r", r=2),
                in0=acc[:].rearrange("p i (r m) -> p i m r", r=2),
                in1=b1_all[:, cols]
                .rearrange("p (m r) -> p m r", r=2)
                .unsqueeze(1)
                .to_broadcast([P, TOKEN_TILES, P, 2]),
                op=ALU.add,
            )

        def statistics(u):
            for i in range(TOKEN_TILES):
                nc.vector.bn_stats(out=stats[:, i, u, :], in_=llm[:, u, i, :])

        w1_copies = (None, None, nc.vector.tensor_copy, nc.scalar.copy)
        first_copies = (None, None, None, nc.scalar.copy)
        w2_copies = (None, None, nc.vector.tensor_copy)

        quantise_unit(transpose_unit(x_raw, PASSES1), x_codes, x_scales, slice(0, TOKENS))
        ready = quantise_w1(transpose_unit(w1_raw[0], PASSES1))

        for c in range(B1_PIECES):
            bank = psum.tile([P, BANK], F32, tag="bank", name="bank")
            nc.tensor.matmul(
                out=bank[:, 0:B1_PIECE], lhsT=select[:, c : c + 1].to_broadcast([P, P]), rhs=b1_rows[:], start=True, stop=True
            )
            nc.vector.tensor_copy(out=b1_all[:, c * B1_PIECE : (c + 1) * B1_PIECE], in_=bank[:, 0:B1_PIECE])

        w1_gathered = None
        w2_gathered = [None] * UNITS
        for u in range(UNITS):
            if u + 1 < UNITS:
                following = quantise_w1(transpose_unit(w1_raw[u + 1], PASSES1, w1_gathered))
            else:
                w2_grouped = [transpose_unit(w2_raw[0], PASSES2, w2_gathered[0])]
            if u + 2 < UNITS:
                w1_gathered = gather_unit(w1_raw[u + 2], PASSES1, w1_copies if u > 0 else first_copies)
            elif u + 1 < UNITS:
                for v in range(2):
                    w2_gathered[v] = gather_unit(w2_raw[v], PASSES2, w2_copies)
            if u > 0:
                statistics(u - 1)
            first_matmul(u, ready[0], ready[1])
            ready = following
        statistics(UNITS - 1)
        for i in range(TOKEN_TILES):
            nc.sync.dma_start(out=llm_out[:, i, :].rearrange("p (u c) -> p u c", c=ROWS), in_=llm[:, :, i, :])

        w2_grouped.append(transpose_unit(w2_raw[1], PASSES2, w2_gathered[1], slice(0, 2)))
        mean_var = keep.tile([P, TOKEN_TILES, 2], F32)
        for i in range(TOKEN_TILES):
            nc.vector.bn_aggr(out=mean_var[:, i, :], in_=stats[:, i, :, :].rearrange("p u s -> p (u s)"))
        quantise_unit(w2_grouped[0][0:1], w2_codes, w2_scales, slice(0, ROWS))
        rstd = keep.tile([P, TOKEN_TILES], F32)
        nc.scalar.activation(
            out=rstd[:], in_=mean_var[:, :, 1], func=ACT.Abs_reciprocal_sqrt, bias=eps[:, 0:1], scale=1.0
        )
        w2_grouped[1].extend(transpose_unit(w2_raw[1], PASSES2, w2_gathered[1], slice(2, PASSES2)))

        xhat = keep.tile([P, TOKEN_TILES, PASSES2, PACK, P], F32)
        for g in range(PASSES2):
            for i in range(TOKEN_TILES):
                source = llm[:, 2 * g : 2 * g + 2, i, :].rearrange("n v (p t) -> n v p t", t=PACK)
                target = xhat[:, i, g, :, :].rearrange("n t (v p) -> n v p t", v=2)
                nc.vector.tensor_scalar(
                    out=target, in0=source, scalar1=mean_var[:, i, 0:1], scalar2=rstd[:, i : i + 1],
                    op0=ALU.subtract, op1=ALU.mult,
                )
        w2_gathered[3] = gather_unit(w2_raw[3], PASSES2, w2_copies)
        w2_grouped.append(transpose_unit(w2_raw[2], PASSES2, w2_gathered[2]))
        quantise_unit(w2_grouped[0][1:3], w2_codes, w2_scales, slice(0, ROWS), 1)
        for v in range(1, 3):
            quantise_w2(v, w2_grouped[v])

        n_codes = keep.tile([P, PASSES2, TOKENS], U32, align_bytes=64)
        n_scales = keep.tile([P, PASSES2, TOKENS], U8, align_bytes=64)
        n_grouped = []
        for g in range(PASSES2):
            planes = stage.tile([P, PACK, TOKENS], BF16, tag="planes", name="planes", bufs=3)
            for u in range(2):
                bank = psum.tile([P, 2, TOKENS], F32, tag="bank", name="bank")
                for e in range(2):
                    for i in range(TOKEN_TILES):
                        nc.tensor.transpose(bank[:, e, i * P : (i + 1) * P], xhat[:, i, g, 2 * u + e, :], ident[:])
                for e in range(2):
                    t = 2 * u + e
                    nc.scalar.activation(
                        out=planes[:, t, :], in_=bank[:, e, :], func=ACT.Identity,
                        scale=gain[:, g, t : t + 1], bias=shift[:, g, t : t + 1],
                    )
            grouped = stage.tile([P, TOKENS * PACK], BF16, align_bytes=64, tag="n_grouped", name="n_grouped", bufs=3)
            nc.vector.tensor_copy(
                out=grouped[:].rearrange("p (r t) -> p r t", t=PACK), in_=planes[:].rearrange("p t r -> p r t")
            )
            n_grouped.append(grouped)
            if g > 0:
                nc.vector.quantize_mx(
                    out=n_codes[:, g - 1, :].bitcast(FP8X4), scales=n_scales[:, g - 1, :], in_=n_grouped[g - 1][:]
                )
        last = PASSES2 - 1
        nc.vector.quantize_mx(out=n_codes[:, last, :].bitcast(FP8X4), scales=n_scales[:, last, :], in_=n_grouped[last][:])

        quantise_w2(3, transpose_unit(w2_raw[3], PASSES2, w2_gathered[3]))

        quantise_w2(4, transpose_unit(w2_raw[4], PASSES2, w2_gathered[4]))
        last_unit = transpose_unit(w2_raw[5], PASSES2, w2_gathered[5])

        q_sb = keep.tile([P, TOKEN_TILES, DIM], F32)

        def second_matmul(i, cols):
            tokens = slice(i * P, (i + 1) * P)
            bank = psum.tile([P, BANK], F32, tag="bank", name="acc")
            acc = bank[:, 0 : cols.stop - cols.start]
            for g in range(PASSES2):
                nc.tensor.matmul_mx(
                    out=acc,
                    lhsT=n_codes[:, g, tokens].bitcast(FP8X4),
                    lhsT_scale=n_scales[:, g, tokens],
                    rhs=w2_codes[:, g, cols].bitcast(FP8X4),
                    rhs_scale=w2_scales[:, g, cols],
                    start=(g == 0),
                    stop=(g == PASSES2 - 1),
                )
            nc.vector.tensor_tensor(
                out=q_sb[:, i, cols].rearrange("p (v m r) -> p v m r", m=P, r=2),
                in0=acc.rearrange("p (v r m) -> p v m r", m=P, r=2),
                in1=qb_all[:, cols].rearrange("p (v m r) -> p v m r", m=P, r=2),
                op=ALU.add,
            )
            nc.sync.dma_start(out=q_out[:, i, cols], in_=q_sb[:, i, cols])

        for c in range(CHUNKS):
            if c == 1:
                quantise_w2(UNITS - 1, last_unit)
            for i in range(TOKEN_TILES):
                width = ROWS if c == CHUNKS - 1 and i == TOKEN_TILES - 1 else BANK
                for first in range(c * BANK, (c + 1) * BANK, width):
                    second_matmul(i, slice(first, first + width))
